import numpy as np
import ml_dtypes


def mxq(x, axis, fmt="e4m3"):
    dtype, down = {"e4m3": (ml_dtypes.float8_e4m3fn, 7), "e5m2": (ml_dtypes.float8_e5m2, 14)}[fmt]
    v = np.moveaxis(np.asarray(x, np.float32).astype(ml_dtypes.bfloat16).astype(np.float64), axis, -1)
    blocks = v.reshape(v.shape[:-1] + (-1, 32))
    amax = np.abs(blocks).max(-1, keepdims=True)
    byte = np.maximum(np.where(amax > 0, np.frexp(amax)[1] - 1 + 127, 0) - down, 1)
    scale = np.exp2(byte - 127.0)
    codes = (blocks / scale).astype(np.float32).astype(dtype).astype(np.float64)
    return np.moveaxis((codes * scale).reshape(v.shape), -1, axis)


WIDE = False


def mx_kscale(k):
    if not WIDE:
        return np.ones(k)
    levels = np.array([10, -10, 5, -5, 0])
    a = np.random.permutation(np.resize(levels, k // 512 * 4)).reshape(k // 512, 4)
    idx = np.arange(k)
    return np.exp2(a[idx // 512, idx % 128 // 32])


BF16 = ml_dtypes.bfloat16


def bf(x):
    return np.asarray(x, np.float32).astype(BF16)


def f64(x):
    return np.asarray(x).astype(np.float64)


E2M1 = np.array([0.0, 0.5, 1.0, 1.5, 2.0, 3.0, 4.0, 6.0, -0.0, -0.5, -1.0, -1.5, -2.0, -3.0, -4.0, -6.0])


def pack_weight(w, fmt):
    k, n = w.shape
    w = f64(bf(w)).reshape(k // 32, 32, n)
    amax = np.abs(w).max(1)
    if fmt == "e4m3":
        byte = np.frexp(amax)[1] - 1 + 127 - 7
    else:
        mant, ex = np.frexp(amax / 6.0)
        byte = np.where(mant > 0.5, ex, ex - 1) + 127
    byte = np.clip(np.where(amax > 0, byte, 1), 1, 254)
    scaled = (w * np.exp2(127.0 - byte)[:, None, :]).reshape(k, n).astype(np.float32)
    by_word = np.ascontiguousarray(scaled.reshape(k // 512, 128, 4, n).transpose(0, 1, 3, 2))
    if fmt == "e4m3":
        words = by_word.astype(ml_dtypes.float8_e4m3fn).view(np.uint8)
    else:
        c = by_word.astype(ml_dtypes.float4_e2m1fn).view(np.uint8) & 0xF
        words = c[..., 0::2] | (c[..., 1::2] << 4)
    return np.ascontiguousarray(words), np.ascontiguousarray(byte.astype(np.uint8).reshape(k // 512, 16, n))


def unpack_weight(words, scales, fmt):
    g, p, n, _ = words.shape
    if fmt == "e4m3":
        vals = np.ascontiguousarray(words).view(ml_dtypes.float8_e4m3fn).astype(np.float64)
    else:
        nib = np.empty((g, p, n, 4), np.uint8)
        nib[..., 0::2] = words & 0xF
        nib[..., 1::2] = words >> 4
        vals = E2M1[nib]
    vals = vals * np.repeat(np.exp2(scales.astype(np.float64) - 127.0), 8, axis=1)[..., None]
    return vals.transpose(0, 1, 3, 2).reshape(g * 512, n)


B, IN_DIM, HID, ATT = 4096, 128, 512, 384
TOTAL = IN_DIM + HID + ATT


def softplus(v):
    return np.logaddexp(v, 0.0)


def sigmoid(v):
    return 1.0 / (1.0 + np.exp(-v))


def setup_inputs():
    s = np.array(mx_kscale(TOTAL), np.float64)
    s[IN_DIM:IN_DIM + HID] = 1.0
    h_ltc = bf(np.random.standard_normal((B, HID)))
    x_t = bf(np.random.standard_normal((B, IN_DIM)) * s[:IN_DIM])
    context = bf(np.random.standard_normal((B, ATT)) * s[IN_DIM + HID:])
    w_gd = np.random.uniform(-1.0, 1.0, (2 * HID, TOTAL)) * 3.0 / np.sqrt(TOTAL) / s[None, :]
    W_gd_words, W_gd_scales = pack_weight(np.ascontiguousarray(w_gd.T), "e4m3")
    return {"t": 0.0,
            "h_ltc": h_ltc,
            "x_t": x_t,
            "context": context,
            "W_gd_words": W_gd_words,
            "W_gd_scales": W_gd_scales,
            "b_gd": bf(np.random.uniform(-0.1, 0.1, (2 * HID,))),
            "W_tau": bf(np.random.uniform(-1.0, 1.0, (HID, HID)) * 2.0 / np.sqrt(HID)),
            "b_tau": bf(np.random.uniform(-0.1, 0.1, (HID,))),
            "gleak": bf(np.random.uniform(0.001, 1.0, (HID,))),
            "cm": bf(np.random.uniform(0.4, 0.6, (HID,)))}


def reference(t, h_ltc, x_t, context, W_gd_words, W_gd_scales, b_gd, W_tau, b_tau, gleak, cm):
    h = f64(h_ltc)
    combined = np.concatenate([f64(x_t), h, f64(context)], axis=1)
    g_d = (mxq(combined, 1, "e4m3") @ unpack_weight(W_gd_words, W_gd_scales, "e4m3")) + f64(b_gd)
    gate, dynamics = np.split(g_d, 2, axis=1)
    tau = softplus(h @ f64(W_tau).T + f64(b_tau))
    numerator = sigmoid(gate) * np.tanh(dynamics) - h
    denominator = tau + softplus(f64(cm)) + softplus(f64(gleak))
    return numerator / (denominator + 1e-6)

@@ -1,0 +1,295 @@
+from contextlib import ExitStack
+
+import concourse.mybir as mybir
+from concourse.masks import make_identity
+
+F32 = mybir.dt.float32
+BF16 = mybir.dt.bfloat16
+U8 = mybir.dt.uint8
+U32 = mybir.dt.uint32
+I32 = mybir.dt.int32
+FP8X4 = mybir.dt.float8_e4m3fn_x4
+ACT = mybir.ActivationFunctionType
+ALU = mybir.AluOpType
+
+B, IN_DIM, HID, ATT = 4096, 128, 512, 384
+FLOPS = 2 * B * (IN_DIM + HID + ATT) * 2 * HID + 2 * B * HID * HID
+
+P = 128
+PACK = 4
+GROUP_ROWS = 512
+ROW_TILES = GROUP_ROWS // P
+GROUPS = B // GROUP_ROWS
+BATCH = 2
+BATCHES = GROUPS // BATCH
+H_PASS, X_PASS = 0, 1
+N_TILES = HID // P
+CLAMP = 32.0
+AHEAD = 2
+F_LN = 4
+LOOK = 2
+MX_BANKS = 4
+
+
+def tile_ltcattentioncell_kernel(
+    tc, t, h_ltc, x_t, context, W_gd_words, W_gd_scales, b_gd, W_tau, b_tau, gleak, cm, out
+):
+    nc = tc.nc
+    with ExitStack() as ctx:
+        ctx.enter_context(tc.manual_schedule())
+        const = ctx.enter_context(tc.tile_pool(name="const", bufs=1))
+        rows = ctx.enter_context(tc.tile_pool(name="rows", bufs=1))
+        work = ctx.enter_context(tc.tile_pool(name="work", bufs=1))
+        psum = ctx.enter_context(tc.psum_pool(name="psum", bufs=8 - MX_BANKS))
+
+        h_groups = h_ltc.rearrange("(g p r) k -> g p r k", p=P, r=ROW_TILES)
+        x_groups = x_t.rearrange("(g p r) k -> g p r k", p=P, r=ROW_TILES)
+        c_groups = context.rearrange("(g p r) k -> g p r k", p=P, r=ROW_TILES)
+        out_groups = out.rearrange("(g p r) j -> g p r j", p=P, r=ROW_TILES)
+
+        h_sb, xc_sb, grouped, codes, planes, tau, soft, product, gate_ps, dyn_ps = {}, {}, {}, {}, {}, {}, {}, {}, {}, {}
+
+        ident_f32 = const.tile([P, P], F32, name="ident_f32")
+        ident_bf16 = const.tile([P, P], BF16, name="ident_bf16")
+        ones_bf16 = const.tile([P, P], BF16, name="ones_bf16")
+        tau_bias_rows = const.tile([P, HID], BF16, name="tau_bias_rows")
+        vec_rows = const.tile([P, P], BF16, name="vec_rows")
+        vec_cols = const.tile([P, 16], F32, name="vec_cols")
+        soft_cols = const.tile([P, 8], F32, name="soft_cols")
+        c_cols = const.tile([P, N_TILES], F32, name="c_cols")
+        half_gate_bias = const.tile([P, N_TILES], F32, name="half_gate_bias")
+        w_planes = const.tile([P, 2, 2 * HID], U8, name="w_planes", align_bytes=64)
+        w_words = const.tile([P, 2, 2 * HID], U32, name="w_words", align_bytes=64)
+        wtau_sb = const.tile([P, N_TILES, HID], BF16, name="wtau_sb")
+        wtau_t = const.tile([P, PACK, HID], BF16, name="wtau_t")
+        c_bc = const.tile([P, HID], F32, name="c_bc")
+
+        nc.vector.memset(vec_rows[:], 0.0)
+        nc.vector.memset(tau_bias_rows[:], 0.0)
+        nc.vector.memset(tau_bias_rows[32:64, :], -CLAMP / 32.0)
+        nc.vector.memset(ones_bf16[:], 1.0)
+        nc.vector.memset(w_planes[:].rearrange("p a n -> p (a n)").bitcast(I32), 0)
+        make_identity(nc, ident_bf16[:])
+        make_identity(nc, ident_f32[:])
+
+        def load_rows(g):
+            h_sb[g] = rows.tile([P, ROW_TILES, HID], BF16, name="h_sb", bufs=7)
+            xc_sb[g] = rows.tile([P, ROW_TILES, HID], BF16, name="xc_sb", bufs=4)
+            nc.sync.dma_start(out=h_sb[g][:], in_=h_groups[g])
+            nc.sync.dma_start(out=xc_sb[g][:, :, 0:IN_DIM], in_=x_groups[g])
+            nc.sync.dma_start(out=xc_sb[g][:, :, IN_DIM:HID], in_=c_groups[g])
+
+        nc.sync.dma_start(out=vec_rows[0:8, :], in_=b_gd.rearrange("(r p) -> r p", p=P))
+        nc.sync.dma_start(out=vec_rows[8:12, :], in_=cm.rearrange("(r p) -> r p", p=P))
+        nc.sync.dma_start(out=vec_rows[12:16, :], in_=gleak.rearrange("(r p) -> r p", p=P))
+        nc.sync.dma_start(out=wtau_sb[:], in_=W_tau.rearrange("(c p) i -> p c i", p=P))
+        nc.sync.dma_start(out=tau_bias_rows[0:1, :], in_=b_tau.rearrange("(o n) -> o n", o=1))
+        load_rows(0)
+        load_rows(1)
+        load_rows(2)
+        load_rows(3)
+
+        word_rows = W_gd_words.rearrange("g p n t -> g p (n t)").bitcast(I32)
+        X_PARTS = IN_DIM // PACK
+        w_int = w_words[:].bitcast(I32)
+        nc.sync.dma_start(out=w_int[0 : P - X_PARTS, H_PASS, :], in_=word_rows[0, X_PARTS:P, :])
+        nc.sync.dma_start(out=w_int[P - X_PARTS : P, H_PASS, :], in_=word_rows[1, 0:X_PARTS, :])
+        nc.sync.dma_start(out=w_int[0:X_PARTS, X_PASS, :], in_=word_rows[0, 0:X_PARTS, :])
+        nc.sync.dma_start(out=w_int[X_PARTS:P, X_PASS, :], in_=word_rows[1, X_PARTS:P, :])
+        scale_rows = W_gd_scales.bitcast(I32)
+        plane_int = w_planes[:].bitcast(I32)
+        for quad in range(4):
+            src_h = scale_rows[0, 4 * (quad + 1) : 4 * (quad + 2), :] if quad < 3 else scale_rows[1, 0:4, :]
+            src_x = scale_rows[0, 0:4, :] if quad == 0 else scale_rows[1, 4 * quad : 4 * quad + 4, :]
+            nc.sync.dma_start(out=plane_int[32 * quad : 32 * quad + 4, H_PASS, :], in_=src_h)
+            nc.sync.dma_start(out=plane_int[32 * quad : 32 * quad + 4, X_PASS, :], in_=src_x)
+
+        vec_ps = psum.tile([P, P], BF16, name="bank")
+        nc.tensor.transpose(out=vec_ps[:], in_=vec_rows[:], identity=ident_bf16[:])
+        nc.vector.tensor_copy(out=vec_cols[:], in_=vec_ps[:, 0:16])
+        nc.vector.tensor_scalar(out=half_gate_bias[:], in0=vec_cols[:, 0:N_TILES], scalar1=0.5, scalar2=None, op0=ALU.mult)
+        nc.vector.tensor_scalar(out=soft_cols[:], in0=vec_cols[:, 8:16], scalar1=CLAMP, scalar2=None, op0=ALU.min)
+        nc.scalar.activation(out=soft_cols[:], in_=soft_cols[:], func=ACT.Exp)
+        nc.scalar.activation(out=soft_cols[:], in_=soft_cols[:], func=ACT.Ln, bias=1.0)
+        nc.vector.tensor_tensor(out=soft_cols[:], in0=soft_cols[:], in1=vec_cols[:, 8:16], op=ALU.max)
+        nc.vector.scalar_tensor_tensor(
+            out=c_cols[:], in0=soft_cols[:, 0:4], scalar=1e-6, in1=soft_cols[:, 4:8], op0=ALU.add, op1=ALU.add
+        )
+
+        for half in range(2):
+            wt_ps = psum.tile([P, 2, HID], BF16, name="bank")
+            for t2 in range(2):
+                for c in range(N_TILES):
+                    nc.tensor.transpose(
+                        out=wt_ps[:, t2, c * P : (c + 1) * P],
+                        in_=wtau_sb[:, c, 2 * half + t2 : HID : PACK],
+                        identity=ident_bf16[:],
+                    )
+            nc.vector.tensor_copy(out=wtau_t[:, 2 * half : 2 * half + 2, :], in_=wt_ps[:])
+
+        c_ps = psum.tile([P, HID], F32, name="bank")
+        for q in range(N_TILES):
+            nc.tensor.transpose(
+                out=c_ps[:, q * P : (q + 1) * P], in_=c_cols[:, q : q + 1].to_broadcast([P, P]), identity=ident_f32[:]
+            )
+        nc.vector.tensor_copy(out=c_bc[:], in_=c_ps[:])
+
+        def new_group(g):
+            grouped[g] = work.tile([P, 2, GROUP_ROWS, PACK], BF16, name="grouped", bufs=2, align_bytes=64)
+
+        def transpose_rows(i):
+            g, r = divmod(i, ROW_TILES)
+            if r == 0:
+                new_group(g)
+            words_ps = psum.tile([P, 2, 2, P], F32, name="bank")
+            for a, src in enumerate((h_sb[g], xc_sb[g])):
+                pairs = src[:, r, :].bitcast(F32)
+                for u in range(2):
+                    nc.tensor.transpose(out=words_ps[:, a, u, :], in_=pairs[:, u : HID // 2 : 2], identity=ident_f32[:])
+            nc.vector.tensor_copy(
+                out=grouped[g][:].bitcast(F32)[:, :, r * P : (r + 1) * P, :],
+                in_=words_ps[:].rearrange("p a u b -> p a b u"),
+            )
+
+        def tau_rows(i):
+            g, r = divmod(i, ROW_TILES)
+            if r == 0:
+                tau[g] = work.tile([P, ROW_TILES, HID], F32, name="tau", bufs=7)
+                soft[g] = work.tile([P, ROW_TILES, HID], F32, name="soft", bufs=4)
+            tau_ps = psum.tile([P, HID], F32, name="bank")
+            nc.tensor.matmul(out=tau_ps[:], lhsT=ones_bf16[:], rhs=tau_bias_rows[:], start=True, stop=False)
+            for t4 in range(PACK):
+                nc.tensor.matmul(
+                    out=tau_ps[:],
+                    lhsT=grouped[g][:, H_PASS, r * P : (r + 1) * P, t4],
+                    rhs=wtau_t[:, t4, :],
+                    start=False,
+                    stop=(t4 == PACK - 1),
+                )
+            nc.vector.tensor_scalar(out=soft[g][:, r, :], in0=tau_ps[:], scalar1=0.0, scalar2=None, op0=ALU.min)
+            nc.vector.scalar_tensor_tensor(
+                out=tau[g][:, r, :], in0=tau_ps[:], scalar=0.0, in1=c_bc[:], op0=ALU.max, op1=ALU.add
+            )
+
+        def front(i):
+            g, r = divmod(i, ROW_TILES)
+            if i + AHEAD < GROUPS * ROW_TILES:
+                transpose_rows(i + AHEAD)
+            tau_rows(i)
+            if r == ROW_TILES - 1:
+                codes[g] = work.tile([P, 2 * GROUP_ROWS], U32, name="codes", bufs=4, align_bytes=64)
+                planes[g] = work.tile([P, 2 * GROUP_ROWS], U8, name="planes", bufs=4, align_bytes=64)
+                nc.vector.quantize_mx(
+                    out=codes[g][:].bitcast(FP8X4),
+                    scales=planes[g][:],
+                    in_=grouped[g][:].rearrange("p a b t -> p (a b t)"),
+                )
+
+        def exponential(g, r):
+            nc.scalar.activation(out=soft[g][:, r, :], in_=soft[g][:, r, :], func=ACT.Exp, bias=CLAMP)
+
+        def softplus_rows(g, r):
+            nc.scalar.activation(out=soft[g][:, r, :], in_=soft[g][:, r, :], func=ACT.Ln, bias=1.0)
+            adder = nc.vector if r % 2 == 1 else nc.gpsimd
+            adder.tensor_tensor(out=tau[g][:, r, :], in0=soft[g][:, r, :], in1=tau[g][:, r, :], op=ALU.add)
+
+        def log_denominator(g, r):
+            nc.scalar.activation(out=tau[g][:, r, :], in_=tau[g][:, r, :], func=ACT.Ln)
+
+        def reciprocal(g, r):
+            nc.scalar.activation(out=tau[g][:, r, :], in_=tau[g][:, r, :], func=ACT.Exp, scale=-1.0)
+
+        def mx_tile(g, n):
+            mx_ps = psum.tile([P, GROUP_ROWS], F32, name="mx_ps", bufs=MX_BANKS)
+            for a in (H_PASS, X_PASS):
+                nc.tensor.matmul_mx(
+                    out=mx_ps[:],
+                    lhsT=w_words[:, a, n * P : (n + 1) * P].bitcast(FP8X4),
+                    lhsT_scale=w_planes[:, a, n * P : (n + 1) * P],
+                    rhs=codes[g][:, a * GROUP_ROWS : (a + 1) * GROUP_ROWS].bitcast(FP8X4),
+                    rhs_scale=planes[g][:, a * GROUP_ROWS : (a + 1) * GROUP_ROWS],
+                    start=(a == H_PASS),
+                    stop=(a == X_PASS),
+                )
+            return mx_ps
+
+        def mx_pair(g, c):
+            gate_ps[g, c] = mx_tile(g, c)
+            dyn_ps[g, c] = mx_tile(g, N_TILES + c)
+
+        def tanh_product(g, c):
+            if c == 0:
+                product[g] = work.tile([P, N_TILES, GROUP_ROWS], F32, name="product", bufs=2)
+            tanh_gate = work.tile([P, GROUP_ROWS], F32, name="tanh_gate", bufs=3)
+            tanh_dyn = work.tile([P, GROUP_ROWS], F32, name="tanh_dyn", bufs=3)
+            nc.scalar.activation(
+                out=tanh_gate[:], in_=gate_ps[g, c][:], func=ACT.Tanh, bias=half_gate_bias[:, c : c + 1], scale=0.5
+            )
+            nc.scalar.activation(
+                out=tanh_dyn[:], in_=dyn_ps[g, c][:], func=ACT.Tanh, bias=vec_cols[:, N_TILES + c : N_TILES + c + 1]
+            )
+            nc.vector.scalar_tensor_tensor(
+                out=product[g][:, c, :], in0=tanh_gate[:], scalar=1.0, in1=tanh_dyn[:], op0=ALU.add, op1=ALU.mult
+            )
+
+        def finish_rows(g, r):
+            back_ps = psum.tile([P, HID], F32, name="bank")
+            for c in range(N_TILES):
+                nc.tensor.transpose(
+                    out=back_ps[:, c * P : (c + 1) * P], in_=product[g][:, c, r * P : (r + 1) * P], identity=ident_f32[:]
+                )
+            numer = work.tile([P, HID], F32, name="numer", bufs=3)
+            nc.vector.scalar_tensor_tensor(
+                out=numer[:], in0=back_ps[:], scalar=0.5, in1=h_sb[g][:, r, :], op0=ALU.mult, op1=ALU.subtract
+            )
+            nc.gpsimd.tensor_tensor(out=tau[g][:, r, :], in0=numer[:], in1=tau[g][:, r, :], op=ALU.mult)
+            if r == ROW_TILES - 1:
+                nc.sync.dma_start(out=out_groups[g], in_=tau[g][:])
+
+        def batch(k):
+            return range(k * BATCH, (k + 1) * BATCH)
+
+        def row_tiles(k):
+            return [(g, r) for g in batch(k) for r in range(ROW_TILES)] if 0 <= k < BATCHES else []
+
+        TILES = BATCH * ROW_TILES
+        for i in range(AHEAD):
+            transpose_rows(i)
+        for i in range(TILES):
+            front(i)
+            exponential(*divmod(i, ROW_TILES))
+
+        for k in range(BATCHES):
+            for g in batch(k + 2):
+                if g < GROUPS:
+                    load_rows(g)
+            now = row_tiles(k)
+            ahead = list(range((k + 1) * TILES, (k + 2) * TILES)) if k + 1 < BATCHES else []
+            first, second = batch(k)
+            for j in range(TILES):
+                softplus_rows(*now[j])
+                if j % 2 == 1 and j // 2 < min(F_LN, len(ahead)):
+                    front(ahead[j // 2])
+            for i in ahead[TILES // 2 : F_LN]:
+                front(i)
+            for g, r in now:
+                log_denominator(g, r)
+            if k >= 1:
+                for r in range(ROW_TILES):
+                    finish_rows(first - 1, r)
+            for c in range(LOOK):
+                mx_pair(first, c)
+            for j in range(TILES):
+                g, c = now[j]
+                reciprocal(g, c)
+                tanh_product(g, c)
+                if j + LOOK < TILES:
+                    mx_pair(*now[j + LOOK])
+                if F_LN + j < len(ahead):
+                    front(ahead[F_LN + j])
+                if j >= ROW_TILES:
+                    finish_rows(first, j - ROW_TILES)
+                if j < len(ahead):
+                    exponential(*divmod(ahead[j], ROW_TILES))
+        for r in range(ROW_TILES):
+            finish_rows(GROUPS - 1, r)

@@ -22,13 +22,17 @@ ROW_TILES = GROUP_ROWS // P
 GROUPS = B // GROUP_ROWS
 BATCH = 2
 BATCHES = GROUPS // BATCH
+TILES = BATCH * ROW_TILES
+ALL_TILES = GROUPS * ROW_TILES
+FEATURE_TILES = HID // P
 H_PASS, X_PASS = 0, 1
-N_TILES = HID // P
+X_PARTS = IN_DIM // PACK
 CLAMP = 32.0
-AHEAD = 2
-F_LN = 4
-LOOK = 2
+PSUM_BANKS = 8
 MX_BANKS = 4
+MX_AHEAD = MX_BANKS // 2
+TRANSPOSE_AHEAD = 2
+FRONT_IN_LN = 6
 
 
 def tile_ltcattentioncell_kernel(
@@ -40,14 +44,15 @@ def tile_ltcattentioncell_kernel(
         const = ctx.enter_context(tc.tile_pool(name="const", bufs=1))
         rows = ctx.enter_context(tc.tile_pool(name="rows", bufs=1))
         work = ctx.enter_context(tc.tile_pool(name="work", bufs=1))
-        psum = ctx.enter_context(tc.psum_pool(name="psum", bufs=8 - MX_BANKS))
+        psum = ctx.enter_context(tc.psum_pool(name="psum", bufs=PSUM_BANKS - MX_BANKS))
 
         h_groups = h_ltc.rearrange("(g p r) k -> g p r k", p=P, r=ROW_TILES)
         x_groups = x_t.rearrange("(g p r) k -> g p r k", p=P, r=ROW_TILES)
         c_groups = context.rearrange("(g p r) k -> g p r k", p=P, r=ROW_TILES)
         out_groups = out.rearrange("(g p r) j -> g p r j", p=P, r=ROW_TILES)
 
-        h_sb, xc_sb, grouped, codes, planes, tau, soft, product, gate_ps, dyn_ps = {}, {}, {}, {}, {}, {}, {}, {}, {}, {}
+        h_sb, xc_sb, grouped, codes, planes, soft, denom, product = {}, {}, {}, {}, {}, {}, {}, {}
+        gate_ps, dyn_ps, numer = {}, {}, {}
 
         ident_f32 = const.tile([P, P], F32, name="ident_f32")
         ident_bf16 = const.tile([P, P], BF16, name="ident_bf16")
@@ -56,11 +61,11 @@ def tile_ltcattentioncell_kernel(
         vec_rows = const.tile([P, P], BF16, name="vec_rows")
         vec_cols = const.tile([P, 16], F32, name="vec_cols")
         soft_cols = const.tile([P, 8], F32, name="soft_cols")
-        c_cols = const.tile([P, N_TILES], F32, name="c_cols")
-        half_gate_bias = const.tile([P, N_TILES], F32, name="half_gate_bias")
-        w_planes = const.tile([P, 2, 2 * HID], U8, name="w_planes", align_bytes=64)
+        c_cols = const.tile([P, FEATURE_TILES], F32, name="c_cols")
+        half_gate_bias = const.tile([P, FEATURE_TILES], F32, name="half_gate_bias")
         w_words = const.tile([P, 2, 2 * HID], U32, name="w_words", align_bytes=64)
-        wtau_sb = const.tile([P, N_TILES, HID], BF16, name="wtau_sb")
+        w_planes = const.tile([P, 2, 2 * HID], U8, name="w_planes", align_bytes=64)
+        wtau_sb = const.tile([P, FEATURE_TILES, HID], BF16, name="wtau_sb")
         wtau_t = const.tile([P, PACK, HID], BF16, name="wtau_t")
         c_bc = const.tile([P, HID], F32, name="c_bc")
 
@@ -84,13 +89,10 @@ def tile_ltcattentioncell_kernel(
         nc.sync.dma_start(out=vec_rows[12:16, :], in_=gleak.rearrange("(r p) -> r p", p=P))
         nc.sync.dma_start(out=wtau_sb[:], in_=W_tau.rearrange("(c p) i -> p c i", p=P))
         nc.sync.dma_start(out=tau_bias_rows[0:1, :], in_=b_tau.rearrange("(o n) -> o n", o=1))
-        load_rows(0)
-        load_rows(1)
-        load_rows(2)
-        load_rows(3)
+        for g in range(2 * BATCH):
+            load_rows(g)
 
         word_rows = W_gd_words.rearrange("g p n t -> g p (n t)").bitcast(I32)
-        X_PARTS = IN_DIM // PACK
         w_int = w_words[:].bitcast(I32)
         nc.sync.dma_start(out=w_int[0 : P - X_PARTS, H_PASS, :], in_=word_rows[0, X_PARTS:P, :])
         nc.sync.dma_start(out=w_int[P - X_PARTS : P, H_PASS, :], in_=word_rows[1, 0:X_PARTS, :])
@@ -107,11 +109,12 @@ def tile_ltcattentioncell_kernel(
         vec_ps = psum.tile([P, P], BF16, name="bank")
         nc.tensor.transpose(out=vec_ps[:], in_=vec_rows[:], identity=ident_bf16[:])
         nc.vector.tensor_copy(out=vec_cols[:], in_=vec_ps[:, 0:16])
-        nc.vector.tensor_scalar(out=half_gate_bias[:], in0=vec_cols[:, 0:N_TILES], scalar1=0.5, scalar2=None, op0=ALU.mult)
-        nc.vector.tensor_scalar(out=soft_cols[:], in0=vec_cols[:, 8:16], scalar1=CLAMP, scalar2=None, op0=ALU.min)
+        gate_bias, dyn_bias, cm_gleak = vec_cols[:, 0:4], vec_cols[:, 4:8], vec_cols[:, 8:16]
+        nc.vector.tensor_scalar(out=half_gate_bias[:], in0=gate_bias, scalar1=0.5, scalar2=None, op0=ALU.mult)
+        nc.vector.tensor_scalar(out=soft_cols[:], in0=cm_gleak, scalar1=CLAMP, scalar2=None, op0=ALU.min)
         nc.scalar.activation(out=soft_cols[:], in_=soft_cols[:], func=ACT.Exp)
         nc.scalar.activation(out=soft_cols[:], in_=soft_cols[:], func=ACT.Ln, bias=1.0)
-        nc.vector.tensor_tensor(out=soft_cols[:], in0=soft_cols[:], in1=vec_cols[:, 8:16], op=ALU.max)
+        nc.vector.tensor_tensor(out=soft_cols[:], in0=soft_cols[:], in1=cm_gleak, op=ALU.max)
         nc.vector.scalar_tensor_tensor(
             out=c_cols[:], in0=soft_cols[:, 0:4], scalar=1e-6, in1=soft_cols[:, 4:8], op0=ALU.add, op1=ALU.add
         )
@@ -119,7 +122,7 @@ def tile_ltcattentioncell_kernel(
         for half in range(2):
             wt_ps = psum.tile([P, 2, HID], BF16, name="bank")
             for t2 in range(2):
-                for c in range(N_TILES):
+                for c in range(FEATURE_TILES):
                     nc.tensor.transpose(
                         out=wt_ps[:, t2, c * P : (c + 1) * P],
                         in_=wtau_sb[:, c, 2 * half + t2 : HID : PACK],
@@ -128,21 +131,18 @@ def tile_ltcattentioncell_kernel(
             nc.vector.tensor_copy(out=wtau_t[:, 2 * half : 2 * half + 2, :], in_=wt_ps[:])
 
         c_ps = psum.tile([P, HID], F32, name="bank")
-        for q in range(N_TILES):
+        for q in range(FEATURE_TILES):
             nc.tensor.transpose(
                 out=c_ps[:, q * P : (q + 1) * P], in_=c_cols[:, q : q + 1].to_broadcast([P, P]), identity=ident_f32[:]
             )
         nc.vector.tensor_copy(out=c_bc[:], in_=c_ps[:])
 
-        def new_group(g):
-            grouped[g] = work.tile([P, 2, GROUP_ROWS, PACK], BF16, name="grouped", bufs=2, align_bytes=64)
-
         def transpose_rows(i):
             g, r = divmod(i, ROW_TILES)
             if r == 0:
-                new_group(g)
+                grouped[g] = work.tile([P, 2, GROUP_ROWS, PACK], BF16, name="grouped", bufs=2, align_bytes=64)
             words_ps = psum.tile([P, 2, 2, P], F32, name="bank")
-            for a, src in enumerate((h_sb[g], xc_sb[g])):
+            for a, src in ((H_PASS, h_sb[g]), (X_PASS, xc_sb[g])):
                 pairs = src[:, r, :].bitcast(F32)
                 for u in range(2):
                     nc.tensor.transpose(out=words_ps[:, a, u, :], in_=pairs[:, u : HID // 2 : 2], identity=ident_f32[:])
@@ -154,50 +154,49 @@ def tile_ltcattentioncell_kernel(
         def tau_rows(i):
             g, r = divmod(i, ROW_TILES)
             if r == 0:
-                tau[g] = work.tile([P, ROW_TILES, HID], F32, name="tau", bufs=7)
                 soft[g] = work.tile([P, ROW_TILES, HID], F32, name="soft", bufs=4)
-            tau_ps = psum.tile([P, HID], F32, name="bank")
-            nc.tensor.matmul(out=tau_ps[:], lhsT=ones_bf16[:], rhs=tau_bias_rows[:], start=True, stop=False)
+                denom[g] = work.tile([P, ROW_TILES, HID], F32, name="denom", bufs=6)
+            z_ps = psum.tile([P, HID], F32, name="bank")
+            nc.tensor.matmul(out=z_ps[:], lhsT=ones_bf16[:], rhs=tau_bias_rows[:], start=True, stop=False)
             for t4 in range(PACK):
                 nc.tensor.matmul(
-                    out=tau_ps[:],
+                    out=z_ps[:],
                     lhsT=grouped[g][:, H_PASS, r * P : (r + 1) * P, t4],
                     rhs=wtau_t[:, t4, :],
                     start=False,
                     stop=(t4 == PACK - 1),
                 )
-            nc.vector.tensor_scalar(out=soft[g][:, r, :], in0=tau_ps[:], scalar1=0.0, scalar2=None, op0=ALU.min)
+            nc.vector.tensor_scalar(out=soft[g][:, r, :], in0=z_ps[:], scalar1=0.0, scalar2=None, op0=ALU.min)
             nc.vector.scalar_tensor_tensor(
-                out=tau[g][:, r, :], in0=tau_ps[:], scalar=0.0, in1=c_bc[:], op0=ALU.max, op1=ALU.add
+                out=denom[g][:, r, :], in0=z_ps[:], scalar=0.0, in1=c_bc[:], op0=ALU.max, op1=ALU.add
             )
 
         def front(i):
-            g, r = divmod(i, ROW_TILES)
-            if i + AHEAD < GROUPS * ROW_TILES:
-                transpose_rows(i + AHEAD)
             tau_rows(i)
-            if r == ROW_TILES - 1:
-                codes[g] = work.tile([P, 2 * GROUP_ROWS], U32, name="codes", bufs=4, align_bytes=64)
-                planes[g] = work.tile([P, 2 * GROUP_ROWS], U8, name="planes", bufs=4, align_bytes=64)
-                nc.vector.quantize_mx(
-                    out=codes[g][:].bitcast(FP8X4),
-                    scales=planes[g][:],
-                    in_=grouped[g][:].rearrange("p a b t -> p (a b t)"),
-                )
+            if i + TRANSPOSE_AHEAD < ALL_TILES:
+                transpose_rows(i + TRANSPOSE_AHEAD)
+
+        def quantise(g):
+            codes[g] = work.tile([P, 2 * GROUP_ROWS], U32, name="codes", bufs=4, align_bytes=64)
+            planes[g] = work.tile([P, 2 * GROUP_ROWS], U8, name="planes", bufs=4, align_bytes=64)
+            nc.vector.quantize_mx(
+                out=codes[g][:].bitcast(FP8X4),
+                scales=planes[g][:],
+                in_=grouped[g][:].rearrange("p a b t -> p (a b t)"),
+            )
 
         def exponential(g, r):
             nc.scalar.activation(out=soft[g][:, r, :], in_=soft[g][:, r, :], func=ACT.Exp, bias=CLAMP)
 
         def softplus_rows(g, r):
             nc.scalar.activation(out=soft[g][:, r, :], in_=soft[g][:, r, :], func=ACT.Ln, bias=1.0)
-            adder = nc.vector if r % 2 == 1 else nc.gpsimd
-            adder.tensor_tensor(out=tau[g][:, r, :], in0=soft[g][:, r, :], in1=tau[g][:, r, :], op=ALU.add)
+            nc.gpsimd.tensor_tensor(out=denom[g][:, r, :], in0=soft[g][:, r, :], in1=denom[g][:, r, :], op=ALU.add)
 
         def log_denominator(g, r):
-            nc.scalar.activation(out=tau[g][:, r, :], in_=tau[g][:, r, :], func=ACT.Ln)
+            nc.scalar.activation(out=denom[g][:, r, :], in_=denom[g][:, r, :], func=ACT.Ln)
 
         def reciprocal(g, r):
-            nc.scalar.activation(out=tau[g][:, r, :], in_=tau[g][:, r, :], func=ACT.Exp, scale=-1.0)
+            nc.scalar.activation(out=denom[g][:, r, :], in_=denom[g][:, r, :], func=ACT.Exp, scale=-1.0)
 
         def mx_tile(g, n):
             mx_ps = psum.tile([P, GROUP_ROWS], F32, name="mx_ps", bufs=MX_BANKS)
@@ -215,81 +214,98 @@ def tile_ltcattentioncell_kernel(
 
         def mx_pair(g, c):
             gate_ps[g, c] = mx_tile(g, c)
-            dyn_ps[g, c] = mx_tile(g, N_TILES + c)
+            dyn_ps[g, c] = mx_tile(g, FEATURE_TILES + c)
 
         def tanh_product(g, c):
             if c == 0:
-                product[g] = work.tile([P, N_TILES, GROUP_ROWS], F32, name="product", bufs=2)
+                product[g] = work.tile([P, FEATURE_TILES, GROUP_ROWS], F32, name="product", bufs=2)
             tanh_gate = work.tile([P, GROUP_ROWS], F32, name="tanh_gate", bufs=3)
             tanh_dyn = work.tile([P, GROUP_ROWS], F32, name="tanh_dyn", bufs=3)
             nc.scalar.activation(
                 out=tanh_gate[:], in_=gate_ps[g, c][:], func=ACT.Tanh, bias=half_gate_bias[:, c : c + 1], scale=0.5
             )
-            nc.scalar.activation(
-                out=tanh_dyn[:], in_=dyn_ps[g, c][:], func=ACT.Tanh, bias=vec_cols[:, N_TILES + c : N_TILES + c + 1]
-            )
+            nc.scalar.activation(out=tanh_dyn[:], in_=dyn_ps[g, c][:], func=ACT.Tanh, bias=dyn_bias[:, c : c + 1])
             nc.vector.scalar_tensor_tensor(
                 out=product[g][:, c, :], in0=tanh_gate[:], scalar=1.0, in1=tanh_dyn[:], op0=ALU.add, op1=ALU.mult
             )
 
-        def finish_rows(g, r):
+        def numerator_rows(g, r):
             back_ps = psum.tile([P, HID], F32, name="bank")
-            for c in range(N_TILES):
+            for c in range(FEATURE_TILES):
                 nc.tensor.transpose(
                     out=back_ps[:, c * P : (c + 1) * P], in_=product[g][:, c, r * P : (r + 1) * P], identity=ident_f32[:]
                 )
-            numer = work.tile([P, HID], F32, name="numer", bufs=3)
+            numer[g, r] = work.tile([P, HID], F32, name="numer", bufs=4)
             nc.vector.scalar_tensor_tensor(
-                out=numer[:], in0=back_ps[:], scalar=0.5, in1=h_sb[g][:, r, :], op0=ALU.mult, op1=ALU.subtract
+                out=numer[g, r][:], in0=back_ps[:], scalar=0.5, in1=h_sb[g][:, r, :], op0=ALU.mult, op1=ALU.subtract
             )
-            nc.gpsimd.tensor_tensor(out=tau[g][:, r, :], in0=numer[:], in1=tau[g][:, r, :], op=ALU.mult)
-            if r == ROW_TILES - 1:
-                nc.sync.dma_start(out=out_groups[g], in_=tau[g][:])
 
-        def batch(k):
-            return range(k * BATCH, (k + 1) * BATCH)
+        def divide_and_store(g, r):
+            nc.vector.tensor_tensor(out=denom[g][:, r, :], in0=numer[g, r][:], in1=denom[g][:, r, :], op=ALU.mult)
+            nc.sync.dma_start(out=out_groups[g][:, r, :], in_=denom[g][:, r, :])
 
-        def row_tiles(k):
-            return [(g, r) for g in batch(k) for r in range(ROW_TILES)] if 0 <= k < BATCHES else []
-
-        TILES = BATCH * ROW_TILES
-        for i in range(AHEAD):
+        for i in range(TRANSPOSE_AHEAD):
             transpose_rows(i)
         for i in range(TILES):
+            g, r = divmod(i, ROW_TILES)
             front(i)
-            exponential(*divmod(i, ROW_TILES))
+            exponential(g, r)
+            if r == ROW_TILES - 1:
+                quantise(g)
 
         for k in range(BATCHES):
-            for g in batch(k + 2):
-                if g < GROUPS:
-                    load_rows(g)
-            now = row_tiles(k)
-            ahead = list(range((k + 1) * TILES, (k + 2) * TILES)) if k + 1 < BATCHES else []
-            first, second = batch(k)
-            for j in range(TILES):
-                softplus_rows(*now[j])
-                if j % 2 == 1 and j // 2 < min(F_LN, len(ahead)):
-                    front(ahead[j // 2])
-            for i in ahead[TILES // 2 : F_LN]:
-                front(i)
-            for g, r in now:
-                log_denominator(g, r)
-            if k >= 1:
+            first, second = k * BATCH, k * BATCH + 1
+            older = first - 1
+            last = k == BATCHES - 1
+            steps = [(g, q) for g in (first, second) for q in range(ROW_TILES)]
+            next_tiles = [] if last else list(range((k + 1) * TILES, (k + 2) * TILES))
+            if k + 2 < BATCHES:
+                load_rows(first + 2 * BATCH)
+                load_rows(second + 2 * BATCH)
+
+            if k > 0:
                 for r in range(ROW_TILES):
-                    finish_rows(first - 1, r)
-            for c in range(LOOK):
+                    log_denominator(older, r)
+            for g, r in steps:
+                softplus_rows(g, r)
+            for r in range(ROW_TILES):
+                log_denominator(first, r)
+            if last:
+                for r in range(ROW_TILES):
+                    log_denominator(second, r)
+            for c in range(MX_AHEAD):
                 mx_pair(first, c)
-            for j in range(TILES):
-                g, c = now[j]
-                reciprocal(g, c)
-                tanh_product(g, c)
-                if j + LOOK < TILES:
-                    mx_pair(*now[j + LOOK])
-                if F_LN + j < len(ahead):
-                    front(ahead[F_LN + j])
+            for i in next_tiles[:FRONT_IN_LN]:
+                front(i)
+            if k > 0:
+                for r in range(ROW_TILES):
+                    numerator_rows(older, r)
+            if not last:
+                quantise(first + BATCH)
+
+            for j, (g, c) in enumerate(steps):
                 if j >= ROW_TILES:
-                    finish_rows(first, j - ROW_TILES)
-                if j < len(ahead):
-                    exponential(*divmod(ahead[j], ROW_TILES))
-        for r in range(ROW_TILES):
-            finish_rows(GROUPS - 1, r)
+                    numerator_rows(first, j - ROW_TILES)
+                tanh_product(g, c)
+                if j + MX_AHEAD < TILES:
+                    mx_pair(*steps[j + MX_AHEAD])
+                if FRONT_IN_LN + j < len(next_tiles):
+                    front(next_tiles[FRONT_IN_LN + j])
+                if j >= ROW_TILES:
+                    reciprocal(first, j - ROW_TILES)
+                    divide_and_store(first, j - ROW_TILES)
+                elif k > 0:
+                    reciprocal(older, j)
+                    divide_and_store(older, j)
+                if not last:
+                    exponential(*divmod(next_tiles[j], ROW_TILES))
+            if not last:
+                quantise(second + BATCH)
+
+        final = GROUPS - 1
+        for r in range(ROW_TILES + 1):
+            if r < ROW_TILES:
+                reciprocal(final, r)
+                numerator_rows(final, r)
+            if r > 0:
+                divide_and_store(final, r - 1)

@@ -130,13 +130,6 @@ def tile_ltcattentioncell_kernel(
                     )
             nc.vector.tensor_copy(out=wtau_t[:, 2 * half : 2 * half + 2, :], in_=wt_ps[:])
 
-        c_ps = psum.tile([P, HID], F32, name="bank")
-        for q in range(FEATURE_TILES):
-            nc.tensor.transpose(
-                out=c_ps[:, q * P : (q + 1) * P], in_=c_cols[:, q : q + 1].to_broadcast([P, P]), identity=ident_f32[:]
-            )
-        nc.vector.tensor_copy(out=c_bc[:], in_=c_ps[:])
-
         def transpose_rows(i):
             g, r = divmod(i, ROW_TILES)
             if r == 0:
@@ -190,7 +183,8 @@ def tile_ltcattentioncell_kernel(
 
         def softplus_rows(g, r):
             nc.scalar.activation(out=soft[g][:, r, :], in_=soft[g][:, r, :], func=ACT.Ln, bias=1.0)
-            nc.gpsimd.tensor_tensor(out=denom[g][:, r, :], in0=soft[g][:, r, :], in1=denom[g][:, r, :], op=ALU.add)
+            adder = nc.vector if g >= GROUPS - BATCH else nc.gpsimd
+            adder.tensor_tensor(out=denom[g][:, r, :], in0=soft[g][:, r, :], in1=denom[g][:, r, :], op=ALU.add)
 
         def log_denominator(g, r):
             nc.scalar.activation(out=denom[g][:, r, :], in_=denom[g][:, r, :], func=ACT.Ln)
@@ -246,6 +240,12 @@ def tile_ltcattentioncell_kernel(
 
         for i in range(TRANSPOSE_AHEAD):
             transpose_rows(i)
+        c_ps = psum.tile([P, HID], F32, name="bank")
+        for q in range(FEATURE_TILES):
+            nc.tensor.transpose(
+                out=c_ps[:, q * P : (q + 1) * P], in_=c_cols[:, q : q + 1].to_broadcast([P, P]), identity=ident_f32[:]
+            )
+        nc.vector.tensor_copy(out=c_bc[:], in_=c_ps[:])
         for i in range(TILES):
             g, r = divmod(i, ROW_TILES)
             front(i)

@@ -32,6 +32,11 @@ PSUM_BANKS = 8
 MX_BANKS = 4
 MX_AHEAD = MX_BANKS // 2
 TRANSPOSE_AHEAD = 2
+SPREAD = False
+SUB_FROM = 6
+COL_FROM = 6
+EARLY = 1
+VREC = 1
 FRONT_IN_LN = 6
 
 
@@ -59,9 +64,11 @@ def tile_ltcattentioncell_kernel(
         ones_bf16 = const.tile([P, P], BF16, name="ones_bf16")
         tau_bias_rows = const.tile([P, HID], BF16, name="tau_bias_rows")
         vec_rows = const.tile([P, P], BF16, name="vec_rows")
-        vec_cols = const.tile([P, 16], F32, name="vec_cols")
+        vec_cols = const.tile([P, 20], F32, name="vec_cols")
         soft_cols = const.tile([P, 8], F32, name="soft_cols")
         c_cols = const.tile([P, FEATURE_TILES], F32, name="c_cols")
+        tau_cols = const.tile([P, FEATURE_TILES], F32, name="tau_cols")
+        minus_two = const.tile([P, P], BF16, name="minus_two")
         half_gate_bias = const.tile([P, FEATURE_TILES], F32, name="half_gate_bias")
         w_words = const.tile([P, 2, 2 * HID], U32, name="w_words", align_bytes=64)
         w_planes = const.tile([P, 2, 2 * HID], U8, name="w_planes", align_bytes=64)
@@ -87,6 +94,7 @@ def tile_ltcattentioncell_kernel(
         nc.sync.dma_start(out=vec_rows[0:8, :], in_=b_gd.rearrange("(r p) -> r p", p=P))
         nc.sync.dma_start(out=vec_rows[8:12, :], in_=cm.rearrange("(r p) -> r p", p=P))
         nc.sync.dma_start(out=vec_rows[12:16, :], in_=gleak.rearrange("(r p) -> r p", p=P))
+        nc.sync.dma_start(out=vec_rows[16:20, :], in_=b_tau.rearrange("(r p) -> r p", p=P))
         nc.sync.dma_start(out=wtau_sb[:], in_=W_tau.rearrange("(c p) i -> p c i", p=P))
         nc.sync.dma_start(out=tau_bias_rows[0:1, :], in_=b_tau.rearrange("(o n) -> o n", o=1))
         for g in range(2 * BATCH):
@@ -108,7 +116,7 @@ def tile_ltcattentioncell_kernel(
 
         vec_ps = psum.tile([P, P], BF16, name="bank")
         nc.tensor.transpose(out=vec_ps[:], in_=vec_rows[:], identity=ident_bf16[:])
-        nc.vector.tensor_copy(out=vec_cols[:], in_=vec_ps[:, 0:16])
+        nc.vector.tensor_copy(out=vec_cols[:], in_=vec_ps[:, 0:20])
         gate_bias, dyn_bias, cm_gleak = vec_cols[:, 0:4], vec_cols[:, 4:8], vec_cols[:, 8:16]
         nc.vector.tensor_scalar(out=half_gate_bias[:], in0=gate_bias, scalar1=0.5, scalar2=None, op0=ALU.mult)
         nc.vector.tensor_scalar(out=soft_cols[:], in0=cm_gleak, scalar1=CLAMP, scalar2=None, op0=ALU.min)
@@ -118,6 +126,9 @@ def tile_ltcattentioncell_kernel(
         nc.vector.scalar_tensor_tensor(
             out=c_cols[:], in0=soft_cols[:, 0:4], scalar=1e-6, in1=soft_cols[:, 4:8], op0=ALU.add, op1=ALU.add
         )
+
+        nc.vector.tensor_scalar(out=tau_cols[:], in0=vec_cols[:, 16:20], scalar1=-CLAMP, scalar2=None, op0=ALU.add)
+        nc.vector.tensor_scalar(out=minus_two[:], in0=ident_bf16[:], scalar1=-2.0, scalar2=None, op0=ALU.mult)
 
         for half in range(2):
             wt_ps = psum.tile([P, 2, HID], BF16, name="bank")
@@ -150,15 +161,27 @@ def tile_ltcattentioncell_kernel(
                 soft[g] = work.tile([P, ROW_TILES, HID], F32, name="soft", bufs=4)
                 denom[g] = work.tile([P, ROW_TILES, HID], F32, name="denom", bufs=6)
             z_ps = psum.tile([P, HID], F32, name="bank")
-            nc.tensor.matmul(out=z_ps[:], lhsT=ones_bf16[:], rhs=tau_bias_rows[:], start=True, stop=False)
+            by_col = g >= COL_FROM
+            if not by_col:
+                nc.tensor.matmul(out=z_ps[:], lhsT=ones_bf16[:], rhs=tau_bias_rows[:], start=True, stop=False)
             for t4 in range(PACK):
                 nc.tensor.matmul(
                     out=z_ps[:],
                     lhsT=grouped[g][:, H_PASS, r * P : (r + 1) * P, t4],
                     rhs=wtau_t[:, t4, :],
-                    start=False,
-                    stop=(t4 == PACK - 1),
+                    start=(by_col and t4 == 0),
+                    stop=(t4 == PACK - 1 and not by_col),
                 )
+            if by_col:
+                for q in range(FEATURE_TILES):
+                    nc.tensor.matmul(
+                        out=z_ps[:, q * P : (q + 1) * P],
+                        lhsT=tau_cols[:, q : q + 1].to_broadcast([P, P]),
+                        rhs=ident_f32[:],
+                        is_transpose=True,
+                        start=False,
+                        stop=(q == FEATURE_TILES - 1),
+                    )
             nc.vector.tensor_scalar(out=soft[g][:, r, :], in0=z_ps[:], scalar1=0.0, scalar2=None, op0=ALU.min)
             nc.vector.scalar_tensor_tensor(
                 out=denom[g][:, r, :], in0=z_ps[:], scalar=0.0, in1=c_bc[:], op0=ALU.max, op1=ALU.add
@@ -225,6 +248,19 @@ def tile_ltcattentioncell_kernel(
 
         def numerator_rows(g, r):
             back_ps = psum.tile([P, HID], F32, name="bank")
+            if g >= SUB_FROM:
+                nc.tensor.matmul(out=back_ps[:], lhsT=minus_two[:], rhs=h_sb[g][:, r, :], start=True, stop=False)
+                for c in range(FEATURE_TILES):
+                    nc.tensor.matmul(
+                        out=back_ps[:, c * P : (c + 1) * P],
+                        lhsT=product[g][:, c, r * P : (r + 1) * P],
+                        rhs=ident_f32[:],
+                        is_transpose=True,
+                        start=False,
+                        stop=(c == FEATURE_TILES - 1),
+                    )
+                numer[g, r] = back_ps
+                return
             for c in range(FEATURE_TILES):
                 nc.tensor.transpose(
                     out=back_ps[:, c * P : (c + 1) * P], in_=product[g][:, c, r * P : (r + 1) * P], identity=ident_f32[:]
@@ -235,7 +271,12 @@ def tile_ltcattentioncell_kernel(
             )
 
         def divide_and_store(g, r):
-            nc.vector.tensor_tensor(out=denom[g][:, r, :], in0=numer[g, r][:], in1=denom[g][:, r, :], op=ALU.mult)
+            if g >= SUB_FROM:
+                nc.vector.scalar_tensor_tensor(
+                    out=denom[g][:, r, :], in0=numer[g, r][:], scalar=0.5, in1=denom[g][:, r, :], op0=ALU.mult, op1=ALU.mult
+                )
+            else:
+                nc.vector.tensor_tensor(out=denom[g][:, r, :], in0=numer[g, r][:], in1=denom[g][:, r, :], op=ALU.mult)
             nc.sync.dma_start(out=out_groups[g][:, r, :], in_=denom[g][:, r, :])
 
         for i in range(TRANSPOSE_AHEAD):
@@ -252,6 +293,9 @@ def tile_ltcattentioncell_kernel(
             exponential(g, r)
             if r == ROW_TILES - 1:
                 quantise(g)
+                if g == 0 and EARLY:
+                    for early in range(ROW_TILES):
+                        softplus_rows(g, early)
 
         for k in range(BATCHES):
             first, second = k * BATCH, k * BATCH + 1
@@ -263,42 +307,66 @@ def tile_ltcattentioncell_kernel(
                 load_rows(first + 2 * BATCH)
                 load_rows(second + 2 * BATCH)
 
+            shown = [first] if k == 0 else [older, first]
+            if last:
+                shown.append(second)
+            tanh_steps = [(g, c) for g in shown for c in range(FEATURE_TILES)]
+            waiting = first - 2
             if k > 0:
-                for r in range(ROW_TILES):
+                for r in range(VREC if last else 0, ROW_TILES):
                     log_denominator(older, r)
+            if last:
+                for r in range(VREC):
+                    nc.vector.reciprocal(out=denom[older][:, r, :], in_=denom[older][:, r, :])
+                    if r == 0:
+                        for q in range(2 * ROW_TILES):
+                            softplus_rows(*steps[q])
             for g, r in steps:
-                softplus_rows(g, r)
+                if not (g == 0 and EARLY) and not (last and VREC):
+                    softplus_rows(g, r)
             for r in range(ROW_TILES):
                 log_denominator(first, r)
             if last:
                 for r in range(ROW_TILES):
                     log_denominator(second, r)
-            for c in range(MX_AHEAD):
-                mx_pair(first, c)
+            for step in tanh_steps[:MX_AHEAD]:
+                mx_pair(*step)
             for i in next_tiles[:FRONT_IN_LN]:
                 front(i)
             if k > 0:
                 for r in range(ROW_TILES):
-                    numerator_rows(older, r)
+                    numerator_rows(waiting, r)
             if not last:
                 quantise(first + BATCH)
 
-            for j, (g, c) in enumerate(steps):
-                if j >= ROW_TILES:
-                    numerator_rows(first, j - ROW_TILES)
+            recs = ([(older, r) for r in range(VREC if last else 0, ROW_TILES)] if k > 0 else []) + [(first, r) for r in range(ROW_TILES)]
+            stores = [(waiting, r) for r in range(ROW_TILES)] if k > 0 else []
+            backs = []
+            n = len(tanh_steps)
+            done = 0
+            nrec = 0
+            for j, (g, c) in enumerate(tanh_steps):
+                if backs:
+                    numerator_rows(*backs[0])
+                    stores.append(backs.pop(0))
                 tanh_product(g, c)
-                if j + MX_AHEAD < TILES:
-                    mx_pair(*steps[j + MX_AHEAD])
-                if FRONT_IN_LN + j < len(next_tiles):
-                    front(next_tiles[FRONT_IN_LN + j])
-                if j >= ROW_TILES:
-                    reciprocal(first, j - ROW_TILES)
-                    divide_and_store(first, j - ROW_TILES)
-                elif k > 0:
-                    reciprocal(older, j)
-                    divide_and_store(older, j)
-                if not last:
-                    exponential(*divmod(next_tiles[j], ROW_TILES))
+                if j + MX_AHEAD < n:
+                    mx_pair(*tanh_steps[j + MX_AHEAD])
+                if c == FEATURE_TILES - 1 and j + 1 < n:
+                    backs += [(g, r) for r in range(ROW_TILES)]
+                fronts = next_tiles[FRONT_IN_LN:]
+                for i in fronts[j * len(fronts) // n : (j + 1) * len(fronts) // n] if SPREAD else fronts[j : j + 1]:
+                    front(i)
+                while nrec < (len(recs) * (j + 1) + n - 1) // n and nrec < len(recs):
+                    reciprocal(*recs[nrec])
+                    nrec += 1
+                if stores and recs.index(stores[0]) < nrec if stores and stores[0] in recs else bool(stores):
+                    divide_and_store(*stores.pop(0))
+                while done < len(next_tiles) * (j + 1) // n:
+                    exponential(*divmod(next_tiles[done], ROW_TILES))
+                    done += 1
+            while stores:
+                divide_and_store(*stores.pop(0))
             if not last:
                 quantise(second + BATCH)
 

@@ -31,8 +31,11 @@ CLAMP = 32.0
 PSUM_BANKS = 8
 MX_BANKS = 4
 MX_AHEAD = MX_BANKS // 2
-TRANSPOSE_AHEAD = 2
+TRANSPOSE_AHEAD = 3
 SPREAD = False
+NU_RUN = 2
+LATE_X = 0
+GRB = 3
 SUB_FROM = 6
 COL_FROM = 6
 EARLY = 1
@@ -122,14 +125,6 @@ def tile_ltcattentioncell_kernel(
         nc.vector.tensor_scalar(out=soft_cols[:], in0=cm_gleak, scalar1=CLAMP, scalar2=None, op0=ALU.min)
         nc.scalar.activation(out=soft_cols[:], in_=soft_cols[:], func=ACT.Exp)
         nc.scalar.activation(out=soft_cols[:], in_=soft_cols[:], func=ACT.Ln, bias=1.0)
-        nc.vector.tensor_tensor(out=soft_cols[:], in0=soft_cols[:], in1=cm_gleak, op=ALU.max)
-        nc.vector.scalar_tensor_tensor(
-            out=c_cols[:], in0=soft_cols[:, 0:4], scalar=1e-6, in1=soft_cols[:, 4:8], op0=ALU.add, op1=ALU.add
-        )
-
-        nc.vector.tensor_scalar(out=tau_cols[:], in0=vec_cols[:, 16:20], scalar1=-CLAMP, scalar2=None, op0=ALU.add)
-        nc.vector.tensor_scalar(out=minus_two[:], in0=ident_bf16[:], scalar1=-2.0, scalar2=None, op0=ALU.mult)
-
         for half in range(2):
             wt_ps = psum.tile([P, 2, HID], BF16, name="bank")
             for t2 in range(2):
@@ -139,12 +134,23 @@ def tile_ltcattentioncell_kernel(
                         in_=wtau_sb[:, c, 2 * half + t2 : HID : PACK],
                         identity=ident_bf16[:],
                     )
-            nc.vector.tensor_copy(out=wtau_t[:, 2 * half : 2 * half + 2, :], in_=wt_ps[:])
+            (nc.scalar.copy if half else nc.vector.tensor_copy)(out=wtau_t[:, 2 * half : 2 * half + 2, :], in_=wt_ps[:])
+
+        nc.vector.tensor_tensor(out=soft_cols[:], in0=soft_cols[:], in1=cm_gleak, op=ALU.max)
+        nc.vector.scalar_tensor_tensor(
+            out=c_cols[:], in0=soft_cols[:, 0:4], scalar=1e-6, in1=soft_cols[:, 4:8], op0=ALU.add, op1=ALU.add
+        )
+        nc.vector.tensor_scalar(out=tau_cols[:], in0=vec_cols[:, 16:20], scalar1=-CLAMP, scalar2=None, op0=ALU.add)
+        nc.vector.tensor_scalar(out=minus_two[:], in0=ident_bf16[:], scalar1=-2.0, scalar2=None, op0=ALU.mult)
 
         def transpose_rows(i):
             g, r = divmod(i, ROW_TILES)
+            if LATE_X and g == 1:
+                if r % 2 == 0:
+                    transpose_half(i, H_PASS)
+                return
             if r == 0:
-                grouped[g] = work.tile([P, 2, GROUP_ROWS, PACK], BF16, name="grouped", bufs=2, align_bytes=64)
+                grouped[g] = work.tile([P, 2, GROUP_ROWS, PACK], BF16, name="grouped", bufs=GRB, align_bytes=64)
             words_ps = psum.tile([P, 2, 2, P], F32, name="bank")
             for a, src in ((H_PASS, h_sb[g]), (X_PASS, xc_sb[g])):
                 pairs = src[:, r, :].bitcast(F32)
@@ -153,6 +159,20 @@ def tile_ltcattentioncell_kernel(
             nc.vector.tensor_copy(
                 out=grouped[g][:].bitcast(F32)[:, :, r * P : (r + 1) * P, :],
                 in_=words_ps[:].rearrange("p a u b -> p a b u"),
+            )
+
+        def transpose_half(i, a):
+            g, r = divmod(i, ROW_TILES)
+            if r == 0 and a == H_PASS:
+                grouped[g] = work.tile([P, 2, GROUP_ROWS, PACK], BF16, name="grouped", bufs=GRB, align_bytes=64)
+            words_ps = psum.tile([P, 2, 2, P], F32, name="bank")
+            for e in range(2):
+                pairs = (h_sb if a == H_PASS else xc_sb)[g][:, r + e, :].bitcast(F32)
+                for u in range(2):
+                    nc.tensor.transpose(out=words_ps[:, e, u, :], in_=pairs[:, u : HID // 2 : 2], identity=ident_f32[:])
+            nc.vector.tensor_copy(
+                out=grouped[g][:].bitcast(F32)[:, a, r * P : (r + 2) * P, :].rearrange("p (e b) u -> p e b u", e=2),
+                in_=words_ps[:].rearrange("p e u b -> p e b u"),
             )
 
         def tau_rows(i):
@@ -279,7 +299,8 @@ def tile_ltcattentioncell_kernel(
                 nc.vector.tensor_tensor(out=denom[g][:, r, :], in0=numer[g, r][:], in1=denom[g][:, r, :], op=ALU.mult)
             nc.sync.dma_start(out=out_groups[g][:, r, :], in_=denom[g][:, r, :])
 
-        for i in range(TRANSPOSE_AHEAD):
+        transpose_half(0, H_PASS)
+        for i in range(2, TRANSPOSE_AHEAD):
             transpose_rows(i)
         c_ps = psum.tile([P, HID], F32, name="bank")
         for q in range(FEATURE_TILES):
@@ -290,9 +311,12 @@ def tile_ltcattentioncell_kernel(
         for i in range(TILES):
             g, r = divmod(i, ROW_TILES)
             front(i)
+            if i == 1:
+                transpose_half(0, X_PASS)
             exponential(g, r)
             if r == ROW_TILES - 1:
-                quantise(g)
+                if g == 0 or not LATE_X:
+                    quantise(g)
                 if g == 0 and EARLY:
                     for early in range(ROW_TILES):
                         softplus_rows(g, early)
@@ -336,6 +360,10 @@ def tile_ltcattentioncell_kernel(
             if k > 0:
                 for r in range(ROW_TILES):
                     numerator_rows(waiting, r)
+            if LATE_X and k == 0:
+                transpose_half(4, X_PASS)
+                transpose_half(6, X_PASS)
+                quantise(1)
             if not last:
                 quantise(first + BATCH)
 
@@ -346,9 +374,10 @@ def tile_ltcattentioncell_kernel(
             done = 0
             nrec = 0
             for j, (g, c) in enumerate(tanh_steps):
-                if backs:
-                    numerator_rows(*backs[0])
-                    stores.append(backs.pop(0))
+                if backs and len(backs) % NU_RUN == 0:
+                    for _ in range(NU_RUN):
+                        numerator_rows(*backs[0])
+                        stores.append(backs.pop(0))
                 tanh_product(g, c)
                 if j + MX_AHEAD < n:
                     mx_pair(*tanh_steps[j + MX_AHEAD])

@@ -33,6 +33,14 @@ MX_BANKS = 4
 MX_AHEAD = MX_BANKS // 2
 TRANSPOSE_AHEAD = 3
 SPREAD = False
+F_AT = 1
+F_STEP = 1
+EARLY_N = 4
+NUM_FIRST = 0
+NU_LAG = 0
+PAIR = 1
+PAIR_HEAD = 0
+FIRST_NU = 0
 NU_RUN = 2
 LATE_X = 0
 GRB = 3
@@ -318,7 +326,7 @@ def tile_ltcattentioncell_kernel(
                 if g == 0 or not LATE_X:
                     quantise(g)
                 if g == 0 and EARLY:
-                    for early in range(ROW_TILES):
+                    for early in range(EARLY_N):
                         softplus_rows(g, early)
 
         for k in range(BATCHES):
@@ -346,7 +354,7 @@ def tile_ltcattentioncell_kernel(
                         for q in range(2 * ROW_TILES):
                             softplus_rows(*steps[q])
             for g, r in steps:
-                if not (g == 0 and EARLY) and not (last and VREC):
+                if not (g == 0 and r < EARLY_N and EARLY) and not (last and VREC):
                     softplus_rows(g, r)
             for r in range(ROW_TILES):
                 log_denominator(first, r)
@@ -355,8 +363,16 @@ def tile_ltcattentioncell_kernel(
                     log_denominator(second, r)
             for step in tanh_steps[:MX_AHEAD]:
                 mx_pair(*step)
-            for i in next_tiles[:FRONT_IN_LN]:
-                front(i)
+            if PAIR:
+                for i in next_tiles[:FRONT_IN_LN:2]:
+                    tau_rows(i)
+                    tau_rows(i + 1)
+                    for ahead in (i + TRANSPOSE_AHEAD, i + 1 + TRANSPOSE_AHEAD):
+                        if ahead < ALL_TILES:
+                            transpose_rows(ahead)
+            else:
+                for i in next_tiles[:FRONT_IN_LN]:
+                    front(i)
             if k > 0:
                 for r in range(ROW_TILES):
                     numerator_rows(waiting, r)
@@ -370,11 +386,12 @@ def tile_ltcattentioncell_kernel(
             recs = ([(older, r) for r in range(VREC if last else 0, ROW_TILES)] if k > 0 else []) + [(first, r) for r in range(ROW_TILES)]
             stores = [(waiting, r) for r in range(ROW_TILES)] if k > 0 else []
             backs = []
+            nu_from = 0
             n = len(tanh_steps)
             done = 0
             nrec = 0
             for j, (g, c) in enumerate(tanh_steps):
-                if backs and len(backs) % NU_RUN == 0:
+                if backs and len(backs) % NU_RUN == 0 and j >= nu_from and (j - nu_from) % NU_RUN == 0:
                     for _ in range(NU_RUN):
                         numerator_rows(*backs[0])
                         stores.append(backs.pop(0))
@@ -383,9 +400,15 @@ def tile_ltcattentioncell_kernel(
                     mx_pair(*tanh_steps[j + MX_AHEAD])
                 if c == FEATURE_TILES - 1 and j + 1 < n:
                     backs += [(g, r) for r in range(ROW_TILES)]
+                    nu_from = j + 1 + NU_LAG
                 fronts = next_tiles[FRONT_IN_LN:]
-                for i in fronts[j * len(fronts) // n : (j + 1) * len(fronts) // n] if SPREAD else fronts[j : j + 1]:
-                    front(i)
+                if j >= F_AT and (j - F_AT) % F_STEP == 0:
+                    fj = (j - F_AT) // F_STEP
+                    for i in fronts[fj : fj + 1]:
+                        front(i)
+                if j == n - 1:
+                    for i in fronts[(j - F_AT) // F_STEP + 1 :]:
+                        front(i)
                 while nrec < (len(recs) * (j + 1) + n - 1) // n and nrec < len(recs):
                     reciprocal(*recs[nrec])
                     nrec += 1
@@ -394,6 +417,9 @@ def tile_ltcattentioncell_kernel(
                 while done < len(next_tiles) * (j + 1) // n:
                     exponential(*divmod(next_tiles[done], ROW_TILES))
                     done += 1
+            for q in backs:
+                numerator_rows(*q)
+                stores.append(q)
             while stores:
                 divide_and_store(*stores.pop(0))
             if not last:

from contextlib import ExitStack

import concourse.mybir as mybir
from concourse.masks import make_identity

F32 = mybir.dt.float32
BF16 = mybir.dt.bfloat16
U8 = mybir.dt.uint8
U32 = mybir.dt.uint32
I32 = mybir.dt.int32
FP8X4 = mybir.dt.float8_e4m3fn_x4
ACT = mybir.ActivationFunctionType
ALU = mybir.AluOpType

B, IN_DIM, HID, ATT = 4096, 128, 512, 384
FLOPS = 2 * B * (IN_DIM + HID + ATT) * 2 * HID + 2 * B * HID * HID

P = 128
PACK = 4
GROUP_ROWS = 512
ROW_TILES = GROUP_ROWS // P
GROUPS = B // GROUP_ROWS
BATCH = 2
BATCHES = GROUPS // BATCH
TILES = BATCH * ROW_TILES
ALL_TILES = GROUPS * ROW_TILES
FEATURE_TILES = HID // P
H_PASS, X_PASS = 0, 1
X_PARTS = IN_DIM // PACK
CLAMP = 32.0
PSUM_BANKS = 8
MX_BANKS = 4
MX_AHEAD = MX_BANKS // 2
TRANSPOSE_AHEAD = 3
SPREAD = False
F_AT = 1
F_STEP = 1
EARLY_N = 4
NUM_FIRST = 0
NU_LAG = 0
PAIR = 1
PAIR_HEAD = 0
FIRST_NU = 0
NU_RUN = 2
LATE_X = 0
GRB = 3
SUB_FROM = 6
COL_FROM = 6
EARLY = 1
VREC = 1
FRONT_IN_LN = 6


def tile_ltcattentioncell_kernel(
    tc, t, h_ltc, x_t, context, W_gd_words, W_gd_scales, b_gd, W_tau, b_tau, gleak, cm, out
):
    nc = tc.nc
    with ExitStack() as ctx:
        ctx.enter_context(tc.manual_schedule())
        const = ctx.enter_context(tc.tile_pool(name="const", bufs=1))
        rows = ctx.enter_context(tc.tile_pool(name="rows", bufs=1))
        work = ctx.enter_context(tc.tile_pool(name="work", bufs=1))
        psum = ctx.enter_context(tc.psum_pool(name="psum", bufs=PSUM_BANKS - MX_BANKS))

        h_groups = h_ltc.rearrange("(g p r) k -> g p r k", p=P, r=ROW_TILES)
        x_groups = x_t.rearrange("(g p r) k -> g p r k", p=P, r=ROW_TILES)
        c_groups = context.rearrange("(g p r) k -> g p r k", p=P, r=ROW_TILES)
        out_groups = out.rearrange("(g p r) j -> g p r j", p=P, r=ROW_TILES)

        h_sb, xc_sb, grouped, codes, planes, soft, denom, product = {}, {}, {}, {}, {}, {}, {}, {}
        gate_ps, dyn_ps, numer = {}, {}, {}

        ident_f32 = const.tile([P, P], F32, name="ident_f32")
        ident_bf16 = const.tile([P, P], BF16, name="ident_bf16")
        ones_bf16 = const.tile([P, P], BF16, name="ones_bf16")
        tau_bias_rows = const.tile([P, HID], BF16, name="tau_bias_rows")
        vec_rows = const.tile([P, P], BF16, name="vec_rows")
        vec_cols = const.tile([P, 20], F32, name="vec_cols")
        soft_cols = const.tile([P, 8], F32, name="soft_cols")
        c_cols = const.tile([P, FEATURE_TILES], F32, name="c_cols")
        tau_cols = const.tile([P, FEATURE_TILES], F32, name="tau_cols")
        minus_two = const.tile([P, P], BF16, name="minus_two")
        half_gate_bias = const.tile([P, FEATURE_TILES], F32, name="half_gate_bias")
        w_words = const.tile([P, 2, 2 * HID], U32, name="w_words", align_bytes=64)
        w_planes = const.tile([P, 2, 2 * HID], U8, name="w_planes", align_bytes=64)
        wtau_sb = const.tile([P, FEATURE_TILES, HID], BF16, name="wtau_sb")
        wtau_t = const.tile([P, PACK, HID], BF16, name="wtau_t")
        c_bc = const.tile([P, HID], F32, name="c_bc")

        nc.vector.memset(vec_rows[:], 0.0)
        nc.vector.memset(tau_bias_rows[:], 0.0)
        nc.vector.memset(tau_bias_rows[32:64, :], -CLAMP / 32.0)
        nc.vector.memset(ones_bf16[:], 1.0)
        nc.vector.memset(w_planes[:].rearrange("p a n -> p (a n)").bitcast(I32), 0)
        make_identity(nc, ident_bf16[:])
        make_identity(nc, ident_f32[:])

        def load_rows(g):
            h_sb[g] = rows.tile([P, ROW_TILES, HID], BF16, name="h_sb", bufs=7)
            xc_sb[g] = rows.tile([P, ROW_TILES, HID], BF16, name="xc_sb", bufs=4)
            nc.sync.dma_start(out=h_sb[g][:], in_=h_groups[g])
            nc.sync.dma_start(out=xc_sb[g][:, :, 0:IN_DIM], in_=x_groups[g])
            nc.sync.dma_start(out=xc_sb[g][:, :, IN_DIM:HID], in_=c_groups[g])

        nc.sync.dma_start(out=vec_rows[0:8, :], in_=b_gd.rearrange("(r p) -> r p", p=P))
        nc.sync.dma_start(out=vec_rows[8:12, :], in_=cm.rearrange("(r p) -> r p", p=P))
        nc.sync.dma_start(out=vec_rows[12:16, :], in_=gleak.rearrange("(r p) -> r p", p=P))
        nc.sync.dma_start(out=vec_rows[16:20, :], in_=b_tau.rearrange("(r p) -> r p", p=P))
        nc.sync.dma_start(out=wtau_sb[:], in_=W_tau.rearrange("(c p) i -> p c i", p=P))
        nc.sync.dma_start(out=tau_bias_rows[0:1, :], in_=b_tau.rearrange("(o n) -> o n", o=1))
        for g in range(2 * BATCH):
            load_rows(g)

        word_rows = W_gd_words.rearrange("g p n t -> g p (n t)").bitcast(I32)
        w_int = w_words[:].bitcast(I32)
        nc.sync.dma_start(out=w_int[0 : P - X_PARTS, H_PASS, :], in_=word_rows[0, X_PARTS:P, :])
        nc.sync.dma_start(out=w_int[P - X_PARTS : P, H_PASS, :], in_=word_rows[1, 0:X_PARTS, :])
        nc.sync.dma_start(out=w_int[0:X_PARTS, X_PASS, :], in_=word_rows[0, 0:X_PARTS, :])
        nc.sync.dma_start(out=w_int[X_PARTS:P, X_PASS, :], in_=word_rows[1, X_PARTS:P, :])
        scale_rows = W_gd_scales.bitcast(I32)
        plane_int = w_planes[:].bitcast(I32)
        for quad in range(4):
            src_h = scale_rows[0, 4 * (quad + 1) : 4 * (quad + 2), :] if quad < 3 else scale_rows[1, 0:4, :]
            src_x = scale_rows[0, 0:4, :] if quad == 0 else scale_rows[1, 4 * quad : 4 * quad + 4, :]
            nc.sync.dma_start(out=plane_int[32 * quad : 32 * quad + 4, H_PASS, :], in_=src_h)
            nc.sync.dma_start(out=plane_int[32 * quad : 32 * quad + 4, X_PASS, :], in_=src_x)

        vec_ps = psum.tile([P, P], BF16, name="bank")
        nc.tensor.transpose(out=vec_ps[:], in_=vec_rows[:], identity=ident_bf16[:])
        nc.vector.tensor_copy(out=vec_cols[:], in_=vec_ps[:, 0:20])
        gate_bias, dyn_bias, cm_gleak = vec_cols[:, 0:4], vec_cols[:, 4:8], vec_cols[:, 8:16]
        nc.vector.tensor_scalar(out=half_gate_bias[:], in0=gate_bias, scalar1=0.5, scalar2=None, op0=ALU.mult)
        nc.vector.tensor_scalar(out=soft_cols[:], in0=cm_gleak, scalar1=CLAMP, scalar2=None, op0=ALU.min)
        nc.scalar.activation(out=soft_cols[:], in_=soft_cols[:], func=ACT.Exp)
        nc.scalar.activation(out=soft_cols[:], in_=soft_cols[:], func=ACT.Ln, bias=1.0)
        for half in range(2):
            wt_ps = psum.tile([P, 2, HID], BF16, name="bank")
            for t2 in range(2):
                for c in range(FEATURE_TILES):
                    nc.tensor.transpose(
                        out=wt_ps[:, t2, c * P : (c + 1) * P],
                        in_=wtau_sb[:, c, 2 * half + t2 : HID : PACK],
                        identity=ident_bf16[:],
                    )
            (nc.scalar.copy if half else nc.vector.tensor_copy)(out=wtau_t[:, 2 * half : 2 * half + 2, :], in_=wt_ps[:])

        nc.vector.tensor_tensor(out=soft_cols[:], in0=soft_cols[:], in1=cm_gleak, op=ALU.max)
        nc.vector.scalar_tensor_tensor(
            out=c_cols[:], in0=soft_cols[:, 0:4], scalar=1e-6, in1=soft_cols[:, 4:8], op0=ALU.add, op1=ALU.add
        )
        nc.vector.tensor_scalar(out=tau_cols[:], in0=vec_cols[:, 16:20], scalar1=-CLAMP, scalar2=None, op0=ALU.add)
        nc.vector.tensor_scalar(out=minus_two[:], in0=ident_bf16[:], scalar1=-2.0, scalar2=None, op0=ALU.mult)

        def transpose_rows(i):
            g, r = divmod(i, ROW_TILES)
            if LATE_X and g == 1:
                if r % 2 == 0:
                    transpose_half(i, H_PASS)
                return
            if r == 0:
                grouped[g] = work.tile([P, 2, GROUP_ROWS, PACK], BF16, name="grouped", bufs=GRB, align_bytes=64)
            words_ps = psum.tile([P, 2, 2, P], F32, name="bank")
            for a, src in ((H_PASS, h_sb[g]), (X_PASS, xc_sb[g])):
                pairs = src[:, r, :].bitcast(F32)
                for u in range(2):
                    nc.tensor.transpose(out=words_ps[:, a, u, :], in_=pairs[:, u : HID // 2 : 2], identity=ident_f32[:])
            nc.vector.tensor_copy(
                out=grouped[g][:].bitcast(F32)[:, :, r * P : (r + 1) * P, :],
                in_=words_ps[:].rearrange("p a u b -> p a b u"),
            )

        def transpose_half(i, a):
            g, r = divmod(i, ROW_TILES)
            if r == 0 and a == H_PASS:
                grouped[g] = work.tile([P, 2, GROUP_ROWS, PACK], BF16, name="grouped", bufs=GRB, align_bytes=64)
            words_ps = psum.tile([P, 2, 2, P], F32, name="bank")
            for e in range(2):
                pairs = (h_sb if a == H_PASS else xc_sb)[g][:, r + e, :].bitcast(F32)
                for u in range(2):
                    nc.tensor.transpose(out=words_ps[:, e, u, :], in_=pairs[:, u : HID // 2 : 2], identity=ident_f32[:])
            nc.vector.tensor_copy(
                out=grouped[g][:].bitcast(F32)[:, a, r * P : (r + 2) * P, :].rearrange("p (e b) u -> p e b u", e=2),
                in_=words_ps[:].rearrange("p e u b -> p e b u"),
            )

        def tau_rows(i):
            g, r = divmod(i, ROW_TILES)
            if r == 0:
                soft[g] = work.tile([P, ROW_TILES, HID], F32, name="soft", bufs=4)
                denom[g] = work.tile([P, ROW_TILES, HID], F32, name="denom", bufs=6)
            z_ps = psum.tile([P, HID], F32, name="bank")
            by_col = g >= COL_FROM
            if not by_col:
                nc.tensor.matmul(out=z_ps[:], lhsT=ones_bf16[:], rhs=tau_bias_rows[:], start=True, stop=False)
            for t4 in range(PACK):
                nc.tensor.matmul(
                    out=z_ps[:],
                    lhsT=grouped[g][:, H_PASS, r * P : (r + 1) * P, t4],
                    rhs=wtau_t[:, t4, :],
                    start=(by_col and t4 == 0),
                    stop=(t4 == PACK - 1 and not by_col),
                )
            if by_col:
                for q in range(FEATURE_TILES):
                    nc.tensor.matmul(
                        out=z_ps[:, q * P : (q + 1) * P],
                        lhsT=tau_cols[:, q : q + 1].to_broadcast([P, P]),
                        rhs=ident_f32[:],
                        is_transpose=True,
                        start=False,
                        stop=(q == FEATURE_TILES - 1),
                    )
            nc.vector.tensor_scalar(out=soft[g][:, r, :], in0=z_ps[:], scalar1=0.0, scalar2=None, op0=ALU.min)
            nc.vector.scalar_tensor_tensor(
                out=denom[g][:, r, :], in0=z_ps[:], scalar=0.0, in1=c_bc[:], op0=ALU.max, op1=ALU.add
            )

        def front(i):
            tau_rows(i)
            if i + TRANSPOSE_AHEAD < ALL_TILES:
                transpose_rows(i + TRANSPOSE_AHEAD)

        def quantise(g):
            codes[g] = work.tile([P, 2 * GROUP_ROWS], U32, name="codes", bufs=4, align_bytes=64)
            planes[g] = work.tile([P, 2 * GROUP_ROWS], U8, name="planes", bufs=4, align_bytes=64)
            nc.vector.quantize_mx(
                out=codes[g][:].bitcast(FP8X4),
                scales=planes[g][:],
                in_=grouped[g][:].rearrange("p a b t -> p (a b t)"),
            )

        def exponential(g, r):
            nc.scalar.activation(out=soft[g][:, r, :], in_=soft[g][:, r, :], func=ACT.Exp, bias=CLAMP)

        def softplus_rows(g, r):
            nc.scalar.activation(out=soft[g][:, r, :], in_=soft[g][:, r, :], func=ACT.Ln, bias=1.0)
            adder = nc.vector if g >= GROUPS - BATCH else nc.gpsimd
            adder.tensor_tensor(out=denom[g][:, r, :], in0=soft[g][:, r, :], in1=denom[g][:, r, :], op=ALU.add)

        def log_denominator(g, r):
            nc.scalar.activation(out=denom[g][:, r, :], in_=denom[g][:, r, :], func=ACT.Ln)

        def reciprocal(g, r):
            nc.scalar.activation(out=denom[g][:, r, :], in_=denom[g][:, r, :], func=ACT.Exp, scale=-1.0)

        def mx_tile(g, n):
            mx_ps = psum.tile([P, GROUP_ROWS], F32, name="mx_ps", bufs=MX_BANKS)
            for a in (H_PASS, X_PASS):
                nc.tensor.matmul_mx(
                    out=mx_ps[:],
                    lhsT=w_words[:, a, n * P : (n + 1) * P].bitcast(FP8X4),
                    lhsT_scale=w_planes[:, a, n * P : (n + 1) * P],
                    rhs=codes[g][:, a * GROUP_ROWS : (a + 1) * GROUP_ROWS].bitcast(FP8X4),
                    rhs_scale=planes[g][:, a * GROUP_ROWS : (a + 1) * GROUP_ROWS],
                    start=(a == H_PASS),
                    stop=(a == X_PASS),
                )
            return mx_ps

        def mx_pair(g, c):
            gate_ps[g, c] = mx_tile(g, c)
            dyn_ps[g, c] = mx_tile(g, FEATURE_TILES + c)

        def tanh_product(g, c):
            if c == 0:
                product[g] = work.tile([P, FEATURE_TILES, GROUP_ROWS], F32, name="product", bufs=2)
            tanh_gate = work.tile([P, GROUP_ROWS], F32, name="tanh_gate", bufs=3)
            tanh_dyn = work.tile([P, GROUP_ROWS], F32, name="tanh_dyn", bufs=3)
            nc.scalar.activation(
                out=tanh_gate[:], in_=gate_ps[g, c][:], func=ACT.Tanh, bias=half_gate_bias[:, c : c + 1], scale=0.5
            )
            nc.scalar.activation(out=tanh_dyn[:], in_=dyn_ps[g, c][:], func=ACT.Tanh, bias=dyn_bias[:, c : c + 1])
            nc.vector.scalar_tensor_tensor(
                out=product[g][:, c, :], in0=tanh_gate[:], scalar=1.0, in1=tanh_dyn[:], op0=ALU.add, op1=ALU.mult
            )

        def numerator_rows(g, r):
            back_ps = psum.tile([P, HID], F32, name="bank")
            if g >= SUB_FROM:
                nc.tensor.matmul(out=back_ps[:], lhsT=minus_two[:], rhs=h_sb[g][:, r, :], start=True, stop=False)
                for c in range(FEATURE_TILES):
                    nc.tensor.matmul(
                        out=back_ps[:, c * P : (c + 1) * P],
                        lhsT=product[g][:, c, r * P : (r + 1) * P],
                        rhs=ident_f32[:],
                        is_transpose=True,
                        start=False,
                        stop=(c == FEATURE_TILES - 1),
                    )
                numer[g, r] = back_ps
                return
            for c in range(FEATURE_TILES):
                nc.tensor.transpose(
                    out=back_ps[:, c * P : (c + 1) * P], in_=product[g][:, c, r * P : (r + 1) * P], identity=ident_f32[:]
                )
            numer[g, r] = work.tile([P, HID], F32, name="numer", bufs=4)
            nc.vector.scalar_tensor_tensor(
                out=numer[g, r][:], in0=back_ps[:], scalar=0.5, in1=h_sb[g][:, r, :], op0=ALU.mult, op1=ALU.subtract
            )

        def divide_and_store(g, r):
            if g >= SUB_FROM:
                nc.vector.scalar_tensor_tensor(
                    out=denom[g][:, r, :], in0=numer[g, r][:], scalar=0.5, in1=denom[g][:, r, :], op0=ALU.mult, op1=ALU.mult
                )
            else:
                nc.vector.tensor_tensor(out=denom[g][:, r, :], in0=numer[g, r][:], in1=denom[g][:, r, :], op=ALU.mult)
            nc.sync.dma_start(out=out_groups[g][:, r, :], in_=denom[g][:, r, :])

        transpose_half(0, H_PASS)
        for i in range(2, TRANSPOSE_AHEAD):
            transpose_rows(i)
        c_ps = psum.tile([P, HID], F32, name="bank")
        for q in range(FEATURE_TILES):
            nc.tensor.transpose(
                out=c_ps[:, q * P : (q + 1) * P], in_=c_cols[:, q : q + 1].to_broadcast([P, P]), identity=ident_f32[:]
            )
        nc.vector.tensor_copy(out=c_bc[:], in_=c_ps[:])
        for i in range(TILES):
            g, r = divmod(i, ROW_TILES)
            front(i)
            if i == 1:
                transpose_half(0, X_PASS)
            exponential(g, r)
            if r == ROW_TILES - 1:
                if g == 0 or not LATE_X:
                    quantise(g)
                if g == 0 and EARLY:
                    for early in range(EARLY_N):
                        softplus_rows(g, early)

        for k in range(BATCHES):
            first, second = k * BATCH, k * BATCH + 1
            older = first - 1
            last = k == BATCHES - 1
            steps = [(g, q) for g in (first, second) for q in range(ROW_TILES)]
            next_tiles = [] if last else list(range((k + 1) * TILES, (k + 2) * TILES))
            if k + 2 < BATCHES:
                load_rows(first + 2 * BATCH)
                load_rows(second + 2 * BATCH)

            shown = [first] if k == 0 else [older, first]
            if last:
                shown.append(second)
            tanh_steps = [(g, c) for g in shown for c in range(FEATURE_TILES)]
            waiting = first - 2
            if k > 0:
                for r in range(VREC if last else 0, ROW_TILES):
                    log_denominator(older, r)
            if last:
                for r in range(VREC):
                    nc.vector.reciprocal(out=denom[older][:, r, :], in_=denom[older][:, r, :])
                    if r == 0:
                        for q in range(2 * ROW_TILES):
                            softplus_rows(*steps[q])
            for g, r in steps:
                if not (g == 0 and r < EARLY_N and EARLY) and not (last and VREC):
                    softplus_rows(g, r)
            for r in range(ROW_TILES):
                log_denominator(first, r)
            if last:
                for r in range(ROW_TILES):
                    log_denominator(second, r)
            for step in tanh_steps[:MX_AHEAD]:
                mx_pair(*step)
            if PAIR:
                for i in next_tiles[:FRONT_IN_LN:2]:
                    tau_rows(i)
                    tau_rows(i + 1)
                    for ahead in (i + TRANSPOSE_AHEAD, i + 1 + TRANSPOSE_AHEAD):
                        if ahead < ALL_TILES:
                            transpose_rows(ahead)
            else:
                for i in next_tiles[:FRONT_IN_LN]:
                    front(i)
            if k > 0:
                for r in range(ROW_TILES):
                    numerator_rows(waiting, r)
            if LATE_X and k == 0:
                transpose_half(4, X_PASS)
                transpose_half(6, X_PASS)
                quantise(1)
            if not last:
                quantise(first + BATCH)

            recs = ([(older, r) for r in range(VREC if last else 0, ROW_TILES)] if k > 0 else []) + [(first, r) for r in range(ROW_TILES)]
            stores = [(waiting, r) for r in range(ROW_TILES)] if k > 0 else []
            backs = []
            nu_from = 0
            n = len(tanh_steps)
            done = 0
            nrec = 0
            for j, (g, c) in enumerate(tanh_steps):
                if backs and len(backs) % NU_RUN == 0 and j >= nu_from and (j - nu_from) % NU_RUN == 0:
                    for _ in range(NU_RUN):
                        numerator_rows(*backs[0])
                        stores.append(backs.pop(0))
                tanh_product(g, c)
                if j + MX_AHEAD < n:
                    mx_pair(*tanh_steps[j + MX_AHEAD])
                if c == FEATURE_TILES - 1 and j + 1 < n:
                    backs += [(g, r) for r in range(ROW_TILES)]
                    nu_from = j + 1 + NU_LAG
                fronts = next_tiles[FRONT_IN_LN:]
                if j >= F_AT and (j - F_AT) % F_STEP == 0:
                    fj = (j - F_AT) // F_STEP
                    for i in fronts[fj : fj + 1]:
                        front(i)
                if j == n - 1:
                    for i in fronts[(j - F_AT) // F_STEP + 1 :]:
                        front(i)
                while nrec < (len(recs) * (j + 1) + n - 1) // n and nrec < len(recs):
                    reciprocal(*recs[nrec])
                    nrec += 1
                if stores and recs.index(stores[0]) < nrec if stores and stores[0] in recs else bool(stores):
                    divide_and_store(*stores.pop(0))
                while done < len(next_tiles) * (j + 1) // n:
                    exponential(*divmod(next_tiles[done], ROW_TILES))
                    done += 1
            for q in backs:
                numerator_rows(*q)
                stores.append(q)
            while stores:
                divide_and_store(*stores.pop(0))
            if not last:
                quantise(second + BATCH)

        final = GROUPS - 1
        for r in range(ROW_TILES + 1):
            if r < ROW_TILES:
                reciprocal(final, r)
                numerator_rows(final, r)
            if r > 0:
                divide_and_store(final, r - 1)
